import numpy as np
import ml_dtypes


BF16 = ml_dtypes.bfloat16


def bf(x):
    return np.asarray(x, np.float32).astype(BF16)


def f64(x):
    return np.asarray(x).astype(np.float64)


E2M1 = np.array([0.0, 0.5, 1.0, 1.5, 2.0, 3.0, 4.0, 6.0, -0.0, -0.5, -1.0, -1.5, -2.0, -3.0, -4.0, -6.0])


def pack_weight(w, fmt):
    k, n = w.shape
    w = f64(bf(w)).reshape(k // 32, 32, n)
    amax = np.abs(w).max(1)
    if fmt == "e4m3":
        byte = np.frexp(amax)[1] - 1 + 127 - 7
    else:
        mant, ex = np.frexp(amax / 6.0)
        byte = np.where(mant > 0.5, ex, ex - 1) + 127
    byte = np.clip(np.where(amax > 0, byte, 1), 1, 254)
    scaled = (w * np.exp2(127.0 - byte)[:, None, :]).reshape(k, n).astype(np.float32)
    by_word = np.ascontiguousarray(scaled.reshape(k // 512, 128, 4, n).transpose(0, 1, 3, 2))
    if fmt == "e4m3":
        words = by_word.astype(ml_dtypes.float8_e4m3fn).view(np.uint8)
    else:
        c = by_word.astype(ml_dtypes.float4_e2m1fn).view(np.uint8) & 0xF
        words = c[..., 0::2] | (c[..., 1::2] << 4)
    return np.ascontiguousarray(words), np.ascontiguousarray(byte.astype(np.uint8).reshape(k // 512, 16, n))


def unpack_weight(words, scales, fmt):
    g, p, n, _ = words.shape
    if fmt == "e4m3":
        vals = np.ascontiguousarray(words).view(ml_dtypes.float8_e4m3fn).astype(np.float64)
    else:
        nib = np.empty((g, p, n, 4), np.uint8)
        nib[..., 0::2] = words & 0xF
        nib[..., 1::2] = words >> 4
        vals = E2M1[nib]
    vals = vals * np.repeat(np.exp2(scales.astype(np.float64) - 127.0), 8, axis=1)[..., None]
    return vals.transpose(0, 1, 3, 2).reshape(g * 512, n)

def pack4(w):
    words, scales = pack_weight(w, "e2m1")
    return words.reshape(words.shape[0], 128, -1), scales


def unpack4(words, scales):
    return unpack_weight(words.reshape(words.shape[0], 128, -1, 2), scales, "e2m1")


def kspread(k):
    return np.exp2(np.repeat(np.random.randint(-6, 7, k // 32), 32).astype(np.float64))


B, S, D, H, KVH, HD = 1, 1024, 8192, 16, 4, 128
THETA = 10000.0


def rope(a, cos, sin):
    a1, a2 = a[..., 0::2], a[..., 1::2]
    c, s = cos[None, None], sin[None, None]
    return np.stack([a1 * c - a2 * s, a1 * s + a2 * c], axis=-1).reshape(a.shape)


def setup_inputs():
    s = kspread(D)
    pos = np.arange(S) + np.random.randint(0, S)
    ang = np.outer(pos, 1.0 / THETA ** (np.arange(0, HD, 2) / HD))
    x = np.random.standard_normal((B, S, D)) * s
    x_words, x_scales = pack4(x.reshape(B * S, D).T)
    Wq_words, Wq_scales = pack4(np.random.standard_normal((D, H * HD)) * 1.5 / np.sqrt(D) / s[:, None])
    Wkv_words, Wkv_scales = pack4(np.random.standard_normal((D, 2 * KVH * HD)) * 1.5 / np.sqrt(D) / s[:, None])
    return {"x_words": x_words, "x_scales": x_scales,
            "cos": bf(np.cos(ang)), "sin": bf(np.sin(ang)),
            "Wq_words": Wq_words, "Wq_scales": Wq_scales,
            "Wkv_words": Wkv_words, "Wkv_scales": Wkv_scales}


def reference(x_words, x_scales, cos, sin, Wq_words, Wq_scales, Wkv_words, Wkv_scales):
    xq = unpack4(x_words, x_scales).T.reshape(B, S, D)
    q = (xq @ unpack4(Wq_words, Wq_scales)).reshape(B, S, H, HD).transpose(0, 2, 1, 3)
    kv = (xq @ unpack4(Wkv_words, Wkv_scales)).reshape(B, S, 2, KVH, HD)
    k = kv[:, :, 0].transpose(0, 2, 1, 3)
    v = kv[:, :, 1].transpose(0, 2, 1, 3)
    return rope(q, f64(cos), f64(sin)), rope(k, f64(cos), f64(sin)), v

@@ -1,0 +1,210 @@
+from contextlib import ExitStack
+
+import concourse.mybir as mybir
+
+F32 = mybir.dt.float32
+BF16 = mybir.dt.bfloat16
+U8 = mybir.dt.uint8
+I32 = mybir.dt.int32
+FP4X4 = mybir.dt.float4_e2m1fn_x4
+MULT = mybir.AluOpType.mult
+ADD = mybir.AluOpType.add
+
+P = 128
+TOKENS = 1024
+K = 8192
+PASSES = K // 512
+M_TILES = TOKENS // P
+N_BLOCK = 512
+HEADS_PER_BLOCK = 4
+PAIRS = 64
+N_BLOCKS = 6
+
+FLOPS = 2 * TOKENS * K * N_BLOCK * N_BLOCKS
+
+W_RUNS = ((0, 4), (4, 8), (8, 16))
+STAGGER_FROM = 13
+WARM_MATMULS = 6
+
+
+def tile_gqa_pa_kernel(
+    tc, x_words, x_scales, cos, sin, Wq_words, Wq_scales, Wkv_words, Wkv_scales, out_0, out_1, out_2
+):
+    nc = tc.nc
+
+    blocks = [(Wq_words, Wq_scales, N_BLOCK * n, out_0, HEADS_PER_BLOCK * n, True) for n in range(4)]
+    blocks.append((Wkv_words, Wkv_scales, 0, out_1, 0, True))
+    blocks.append((Wkv_words, Wkv_scales, N_BLOCK, out_2, 0, False))
+
+    with ExitStack() as ctx:
+        ctx.enter_context(tc.manual_schedule())
+        keep = ctx.enter_context(tc.tile_pool(name="keep", bufs=1))
+        work = ctx.enter_context(tc.tile_pool(name="work", bufs=1))
+        psum = ctx.enter_context(tc.psum_pool(name="psum", bufs=1))
+
+        xc = keep.tile([P, PASSES, 2 * TOKENS], U8, name="xc", tag="xc", align_bytes=64)
+        xs = keep.tile([P, PASSES, TOKENS], U8, name="xs", tag="xs", align_bytes=64)
+        wc = []
+        ws = []
+        for n in range(N_BLOCKS):
+            wc_n = keep.tile([P, PASSES, 2 * N_BLOCK], U8, name="wc%d" % n, tag="wc%d" % n, align_bytes=64)
+            ws_n = keep.tile([P, PASSES, N_BLOCK], U8, name="ws%d" % n, tag="ws%d" % n, align_bytes=64)
+            wc.append(wc_n)
+            ws.append(ws_n)
+        cos_sb = keep.tile([P, M_TILES, PAIRS], BF16, name="cos_sb", tag="cos_sb")
+        sin_sb = keep.tile([P, M_TILES, PAIRS], BF16, name="sin_sb", tag="sin_sb")
+        t_even = keep.tile([P, M_TILES, PAIRS, 2], BF16, name="t_even", tag="t_even")
+        t_odd = keep.tile([P, M_TILES, PAIRS, 2], BF16, name="t_odd", tag="t_odd")
+
+        def zero_planes(plane, g0, g1):
+            nc.vector.memset(plane[:, g0:g1, :].bitcast(I32), 0)
+
+        def load_x_codes(g0, g1, b0=0, b1=2 * TOKENS):
+            nc.sync.dma_start(
+                out=xc[:, g0:g1, b0:b1].bitcast(I32),
+                in_=x_words[g0:g1, :, b0:b1].rearrange("g p b -> p g b").bitcast(I32),
+            )
+
+        def load_w_codes(n, g0, g1):
+            words, c0 = blocks[n][0], blocks[n][2]
+            nc.sync.dma_start(
+                out=wc[n][:, g0:g1, :].bitcast(I32),
+                in_=words[g0:g1, :, 2 * c0 : 2 * (c0 + N_BLOCK)].rearrange("g p b -> p g b").bitcast(I32),
+            )
+
+        def load_scale_quadrant(plane, scales, c0, width, g0, g1, q):
+            nc.sync.dma_start(
+                out=plane[32 * q : 32 * q + 4, g0:g1, :].bitcast(I32),
+                in_=scales[g0:g1, 4 * q : 4 * q + 4, c0 : c0 + width].rearrange("g r n -> r g n").bitcast(I32),
+            )
+
+        def load_x_scales(g0, g1):
+            for q in (0, 2, 1, 3):
+                load_scale_quadrant(xs, x_scales, 0, TOKENS, g0, g1, q)
+
+        def load_w_scales(n, g0, g1):
+            for q in (0, 2, 1, 3):
+                load_scale_quadrant(ws[n], blocks[n][1], blocks[n][2], N_BLOCK, g0, g1, q)
+
+        warm_in = keep.tile([P, N_BLOCK], BF16, name="warm_in", tag="warm_in")
+        nc.gpsimd.memset(xs[:, 0:2, :].bitcast(F32), 0.0)
+        nc.gpsimd.memset(warm_in[:], 0.0)
+        warm_out = psum.tile([P, N_BLOCK], F32, name="acc7", tag="acc7")
+        for i in range(WARM_MATMULS):
+            nc.tensor.matmul(out=warm_out[:], lhsT=warm_in[:, 0:P], rhs=warm_in[:], start=True, stop=True)
+
+        nc.gpsimd.dma_start(out=cos_sb[:], in_=cos.rearrange("(m p) i -> p m i", p=P))
+        nc.gpsimd.dma_start(out=sin_sb[:], in_=sin.rearrange("(m p) i -> p m i", p=P))
+
+        zero_planes(ws[0], 0, 2)
+        for g0 in range(2, PASSES, 2):
+            zero_planes(xs, g0, g0 + 2)
+            zero_planes(ws[0], g0, g0 + 2)
+        for n in range(1, N_BLOCKS):
+            for g0, g1 in W_RUNS:
+                zero_planes(ws[n], g0, g1)
+
+        nc.vector.tensor_copy(out=t_even[:, :, :, 0], in_=cos_sb[:])
+        nc.vector.tensor_copy(out=t_even[:, :, :, 1], in_=sin_sb[:])
+        nc.vector.tensor_scalar_mul(out=t_odd[:, :, :, 0], in0=sin_sb[:], scalar1=-1.0)
+        nc.vector.tensor_copy(out=t_odd[:, :, :, 1], in_=cos_sb[:])
+
+        load_x_codes(0, 1, 0, 4 * P)
+        load_w_codes(0, 0, 1)
+        load_x_scales(0, 2)
+        load_w_scales(0, 0, 2)
+        load_x_codes(0, 1, 4 * P, 2 * TOKENS)
+        load_w_codes(0, 1, 4)
+        load_x_codes(1, 2)
+        load_x_codes(2, 3)
+        load_x_scales(2, 4)
+        load_w_scales(0, 2, 4)
+        load_x_codes(3, 4)
+        for g0 in range(4, PASSES, 2):
+            load_x_scales(g0, g0 + 2)
+            load_w_scales(0, g0, g0 + 2)
+            load_x_codes(g0, g0 + 1)
+            load_w_codes(0, g0, g0 + 2)
+            load_x_codes(g0 + 1, g0 + 2)
+        for n in range(1, N_BLOCKS):
+            for g0, g1 in W_RUNS:
+                load_w_scales(n, g0, g1)
+                for g in range(g0, g1, 4):
+                    load_w_codes(n, g, g + 4)
+
+        order = []
+        for g in range(STAGGER_FROM):
+            for m in range(M_TILES):
+                order.append((m, 0, g))
+        for half in (0, 4):
+            for g in range(STAGGER_FROM, PASSES):
+                for m in range(half, half + 4):
+                    order.append((m, 0, g))
+        for n in range(1, N_BLOCKS - 1):
+            for half in (0, 4):
+                for g in range(PASSES):
+                    for m in range(half, half + 4):
+                        order.append((m, n, g))
+        for m in range(M_TILES - 1):
+            for g in range(PASSES):
+                order.append((m, N_BLOCKS - 1, g))
+
+        full = [P, HEADS_PER_BLOCK, PAIRS, 2]
+        acc = {}
+        for m, n, g in order:
+            if g == 0:
+                acc_mn = psum.tile([P, N_BLOCK], F32, name="acc%d" % m, tag="acc%d" % m)
+                acc[m] = acc_mn
+            nc.tensor.matmul_mx(
+                out=acc[m][:],
+                lhsT=xc[:, g, 2 * P * m : 2 * P * (m + 1)].bitcast(FP4X4),
+                lhsT_scale=xs[:, g, P * m : P * (m + 1)],
+                rhs=wc[n][:, g, :].bitcast(FP4X4),
+                rhs_scale=ws[n][:, g, :],
+                start=(g == 0),
+                stop=(g == PASSES - 1),
+            )
+            if g < PASSES - 1:
+                continue
+            dst, h0, rotated = blocks[n][3], blocks[n][4], blocks[n][5]
+            rows = dst[0, h0 : h0 + HEADS_PER_BLOCK, P * m : P * (m + 1), :].rearrange("h p l -> p h l")
+            a = work.tile(full, F32, name="a", tag="a", bufs=4)
+            nc.scalar.copy(out=a[:].rearrange("p h i j -> p (h i j)"), in_=acc[m][:])
+            if rotated:
+                u = work.tile(full, F32, name="u", tag="u", bufs=4)
+                w = work.tile(full, F32, name="w", tag="w", bufs=2)
+                nc.vector.tensor_tensor(
+                    out=u[:], in0=a[:, :, :, 0:1].to_broadcast(full),
+                    in1=t_even[:, m : m + 1, :, :].to_broadcast(full), op=MULT,
+                )
+                nc.vector.tensor_tensor(
+                    out=w[:], in0=a[:, :, :, 1:2].to_broadcast(full),
+                    in1=t_odd[:, m : m + 1, :, :].to_broadcast(full), op=MULT,
+                )
+                nc.vector.tensor_tensor(out=u[:], in0=u[:], in1=w[:], op=ADD)
+                nc.gpsimd.dma_start(out=rows, in_=u[:].rearrange("p h i j -> p h (i j)"))
+            else:
+                nc.sync.dma_start(out=rows, in_=a[:].rearrange("p h i j -> p h (i j)"))
+
+        m = M_TILES - 1
+        n = N_BLOCKS - 1
+        half_w = N_BLOCK // 2
+        for half in range(2):
+            bank = (m + half) % M_TILES
+            acc_h = psum.tile([P, N_BLOCK], F32, name="acc%d" % bank, tag="acc%d" % bank)
+            for g in range(PASSES):
+                nc.tensor.matmul_mx(
+                    out=acc_h[:, 0:half_w],
+                    lhsT=xc[:, g, 2 * P * m : 2 * P * (m + 1)].bitcast(FP4X4),
+                    lhsT_scale=xs[:, g, P * m : P * (m + 1)],
+                    rhs=wc[n][:, g, 2 * half_w * half : 2 * half_w * (half + 1)].bitcast(FP4X4),
+                    rhs_scale=ws[n][:, g, half_w * half : half_w * (half + 1)],
+                    start=(g == 0),
+                    stop=(g == PASSES - 1),
+                )
+            a = work.tile(full, F32, name="a", tag="a", bufs=4)
+            nc.scalar.copy(out=a[:, 0:2, :, :].rearrange("p h i j -> p (h i j)"), in_=acc_h[:, 0:half_w])
+            nc.scalar.dma_start(
+                out=out_2[0, 2 * half : 2 * half + 2, P * m : P * (m + 1), :].rearrange("h p l -> p h l"),
+                in_=a[:, 0:2, :, :].rearrange("p h i j -> p h (i j)"),
+            )

@@ -93,9 +93,6 @@ def tile_gqa_pa_kernel(
         for i in range(WARM_MATMULS):
             nc.tensor.matmul(out=warm_out[:], lhsT=warm_in[:, 0:P], rhs=warm_in[:], start=True, stop=True)
 
-        nc.gpsimd.dma_start(out=cos_sb[:], in_=cos.rearrange("(m p) i -> p m i", p=P))
-        nc.gpsimd.dma_start(out=sin_sb[:], in_=sin.rearrange("(m p) i -> p m i", p=P))
-
         zero_planes(ws[0], 0, 2)
         for g0 in range(2, PASSES, 2):
             zero_planes(xs, g0, g0 + 2)
@@ -103,11 +100,6 @@ def tile_gqa_pa_kernel(
         for n in range(1, N_BLOCKS):
             for g0, g1 in W_RUNS:
                 zero_planes(ws[n], g0, g1)
-
-        nc.vector.tensor_copy(out=t_even[:, :, :, 0], in_=cos_sb[:])
-        nc.vector.tensor_copy(out=t_even[:, :, :, 1], in_=sin_sb[:])
-        nc.vector.tensor_scalar_mul(out=t_odd[:, :, :, 0], in0=sin_sb[:], scalar1=-1.0)
-        nc.vector.tensor_copy(out=t_odd[:, :, :, 1], in_=cos_sb[:])
 
         load_x_codes(0, 1, 0, 4 * P)
         load_w_codes(0, 0, 1)
@@ -126,11 +118,21 @@ def tile_gqa_pa_kernel(
             load_x_codes(g0, g0 + 1)
             load_w_codes(0, g0, g0 + 2)
             load_x_codes(g0 + 1, g0 + 2)
-        for n in range(1, N_BLOCKS):
+        nc.sync.dma_start(out=cos_sb[:], in_=cos.rearrange("(m p) i -> p m i", p=P))
+        nc.sync.dma_start(out=sin_sb[:], in_=sin.rearrange("(m p) i -> p m i", p=P))
+
+        def load_block(n):
             for g0, g1 in W_RUNS:
                 load_w_scales(n, g0, g1)
                 for g in range(g0, g1, 4):
                     load_w_codes(n, g, g + 4)
+
+        load_block(1)
+
+        nc.vector.tensor_copy(out=t_even[:, :, :, 0], in_=cos_sb[:])
+        nc.vector.tensor_copy(out=t_even[:, :, :, 1], in_=sin_sb[:])
+        nc.vector.tensor_scalar_mul(out=t_odd[:, :, :, 0], in0=sin_sb[:], scalar1=-1.0)
+        nc.vector.tensor_copy(out=t_odd[:, :, :, 1], in_=cos_sb[:])
 
         order = []
         for g in range(STAGGER_FROM):
@@ -151,6 +153,7 @@ def tile_gqa_pa_kernel(
 
         full = [P, HEADS_PER_BLOCK, PAIRS, 2]
         acc = {}
+        finished = {}
         for m, n, g in order:
             if g == 0:
                 acc_mn = psum.tile([P, N_BLOCK], F32, name="acc%d" % m, tag="acc%d" % m)
@@ -182,7 +185,10 @@ def tile_gqa_pa_kernel(
                     in1=t_odd[:, m : m + 1, :, :].to_broadcast(full), op=MULT,
                 )
                 nc.vector.tensor_tensor(out=u[:], in0=u[:], in1=w[:], op=ADD)
-                nc.gpsimd.dma_start(out=rows, in_=u[:].rearrange("p h i j -> p h (i j)"))
+                nc.sync.dma_start(out=rows, in_=u[:].rearrange("p h i j -> p h (i j)"))
+                finished[n] = finished.get(n, 0) + 1
+                if finished[n] == M_TILES and n + 2 < N_BLOCKS:
+                    load_block(n + 2)
             else:
                 nc.sync.dma_start(out=rows, in_=a[:].rearrange("p h i j -> p h (i j)"))
 

@@ -210,7 +210,7 @@ def tile_gqa_pa_kernel(
                 )
             a = work.tile(full, F32, name="a", tag="a", bufs=4)
             nc.scalar.copy(out=a[:, 0:2, :, :].rearrange("p h i j -> p (h i j)"), in_=acc_h[:, 0:half_w])
-            nc.scalar.dma_start(
+            nc.sync.dma_start(
                 out=out_2[0, 2 * half : 2 * half + 2, P * m : P * (m + 1), :].rearrange("h p l -> p h l"),
                 in_=a[:, 0:2, :, :].rearrange("p h i j -> p h (i j)"),
             )

@@ -25,6 +25,7 @@ FLOPS = 2 * TOKENS * K * N_BLOCK * N_BLOCKS
 W_RUNS = ((0, 4), (4, 8), (8, 16))
 STAGGER_FROM = 13
 WARM_MATMULS = 6
+LAST_WIDTHS = (256, 128, 128)
 
 
 def tile_gqa_pa_kernel(
@@ -194,23 +195,26 @@ def tile_gqa_pa_kernel(
 
         m = M_TILES - 1
         n = N_BLOCKS - 1
-        half_w = N_BLOCK // 2
-        for half in range(2):
-            bank = (m + half) % M_TILES
+        c0 = 0
+        for part, width in enumerate(LAST_WIDTHS):
+            bank = (m + part) % M_TILES
+            heads = width // P
             acc_h = psum.tile([P, N_BLOCK], F32, name="acc%d" % bank, tag="acc%d" % bank)
             for g in range(PASSES):
                 nc.tensor.matmul_mx(
-                    out=acc_h[:, 0:half_w],
+                    out=acc_h[:, 0:width],
                     lhsT=xc[:, g, 2 * P * m : 2 * P * (m + 1)].bitcast(FP4X4),
                     lhsT_scale=xs[:, g, P * m : P * (m + 1)],
-                    rhs=wc[n][:, g, 2 * half_w * half : 2 * half_w * (half + 1)].bitcast(FP4X4),
-                    rhs_scale=ws[n][:, g, half_w * half : half_w * (half + 1)],
+                    rhs=wc[n][:, g, 2 * c0 : 2 * (c0 + width)].bitcast(FP4X4),
+                    rhs_scale=ws[n][:, g, c0 : c0 + width],
                     start=(g == 0),
                     stop=(g == PASSES - 1),
                 )
             a = work.tile(full, F32, name="a", tag="a", bufs=4)
-            nc.scalar.copy(out=a[:, 0:2, :, :].rearrange("p h i j -> p (h i j)"), in_=acc_h[:, 0:half_w])
+            nc.scalar.copy(out=a[:, 0:heads, :, :].rearrange("p h i j -> p (h i j)"), in_=acc_h[:, 0:width])
+            h0 = c0 // P
             nc.sync.dma_start(
-                out=out_2[0, 2 * half : 2 * half + 2, P * m : P * (m + 1), :].rearrange("h p l -> p h l"),
-                in_=a[:, 0:2, :, :].rearrange("p h i j -> p h (i j)"),
+                out=out_2[0, h0 : h0 + heads, P * m : P * (m + 1), :].rearrange("h p l -> p h l"),
+                in_=a[:, 0:heads, :, :].rearrange("p h i j -> p h (i j)"),
             )
+            c0 += width

@@ -102,11 +102,10 @@ def tile_gqa_pa_kernel(
             for g0, g1 in W_RUNS:
                 zero_planes(ws[n], g0, g1)
 
-        load_x_codes(0, 1, 0, 4 * P)
+        load_x_codes(0, 1)
         load_w_codes(0, 0, 1)
         load_x_scales(0, 2)
         load_w_scales(0, 0, 2)
-        load_x_codes(0, 1, 4 * P, 2 * TOKENS)
         load_w_codes(0, 1, 4)
         load_x_codes(1, 2)
         load_x_codes(2, 3)

@@ -80,11 +80,11 @@ def tile_gqa_pa_kernel(
             )
 
         def load_x_scales(g0, g1):
-            for q in (0, 2, 1, 3):
+            for q in (0, 1, 2, 3):
                 load_scale_quadrant(xs, x_scales, 0, TOKENS, g0, g1, q)
 
         def load_w_scales(n, g0, g1):
-            for q in (0, 2, 1, 3):
+            for q in (0, 1, 2, 3):
                 load_scale_quadrant(ws[n], blocks[n][1], blocks[n][2], N_BLOCK, g0, g1, q)
 
         warm_in = keep.tile([P, N_BLOCK], BF16, name="warm_in", tag="warm_in")

@@ -24,7 +24,6 @@ FLOPS = 2 * TOKENS * K * N_BLOCK * N_BLOCKS
 
 W_RUNS = ((0, 4), (4, 8), (8, 16))
 STAGGER_FROM = 13
-WARM_MATMULS = 6
 LAST_WIDTHS = (256, 128, 128)
 
 
@@ -87,12 +86,7 @@ def tile_gqa_pa_kernel(
             for q in (0, 1, 2, 3):
                 load_scale_quadrant(ws[n], blocks[n][1], blocks[n][2], N_BLOCK, g0, g1, q)
 
-        warm_in = keep.tile([P, N_BLOCK], BF16, name="warm_in", tag="warm_in")
         nc.gpsimd.memset(xs[:, 0:2, :].bitcast(F32), 0.0)
-        nc.gpsimd.memset(warm_in[:], 0.0)
-        warm_out = psum.tile([P, N_BLOCK], F32, name="acc7", tag="acc7")
-        for i in range(WARM_MATMULS):
-            nc.tensor.matmul(out=warm_out[:], lhsT=warm_in[:, 0:P], rhs=warm_in[:], start=True, stop=True)
 
         zero_planes(ws[0], 0, 2)
         for g0 in range(2, PASSES, 2):

from contextlib import ExitStack

import concourse.mybir as mybir

F32 = mybir.dt.float32
BF16 = mybir.dt.bfloat16
U8 = mybir.dt.uint8
I32 = mybir.dt.int32
FP4X4 = mybir.dt.float4_e2m1fn_x4
MULT = mybir.AluOpType.mult
ADD = mybir.AluOpType.add

P = 128
TOKENS = 1024
K = 8192
PASSES = K // 512
M_TILES = TOKENS // P
N_BLOCK = 512
HEADS_PER_BLOCK = 4
PAIRS = 64
N_BLOCKS = 6

FLOPS = 2 * TOKENS * K * N_BLOCK * N_BLOCKS

W_RUNS = ((0, 4), (4, 8), (8, 16))
STAGGER_FROM = 13
LAST_WIDTHS = (256, 128, 128)


def tile_gqa_pa_kernel(
    tc, x_words, x_scales, cos, sin, Wq_words, Wq_scales, Wkv_words, Wkv_scales, out_0, out_1, out_2
):
    nc = tc.nc

    blocks = [(Wq_words, Wq_scales, N_BLOCK * n, out_0, HEADS_PER_BLOCK * n, True) for n in range(4)]
    blocks.append((Wkv_words, Wkv_scales, 0, out_1, 0, True))
    blocks.append((Wkv_words, Wkv_scales, N_BLOCK, out_2, 0, False))

    with ExitStack() as ctx:
        ctx.enter_context(tc.manual_schedule())
        keep = ctx.enter_context(tc.tile_pool(name="keep", bufs=1))
        work = ctx.enter_context(tc.tile_pool(name="work", bufs=1))
        psum = ctx.enter_context(tc.psum_pool(name="psum", bufs=1))

        xc = keep.tile([P, PASSES, 2 * TOKENS], U8, name="xc", tag="xc", align_bytes=64)
        xs = keep.tile([P, PASSES, TOKENS], U8, name="xs", tag="xs", align_bytes=64)
        wc = []
        ws = []
        for n in range(N_BLOCKS):
            wc_n = keep.tile([P, PASSES, 2 * N_BLOCK], U8, name="wc%d" % n, tag="wc%d" % n, align_bytes=64)
            ws_n = keep.tile([P, PASSES, N_BLOCK], U8, name="ws%d" % n, tag="ws%d" % n, align_bytes=64)
            wc.append(wc_n)
            ws.append(ws_n)
        cos_sb = keep.tile([P, M_TILES, PAIRS], BF16, name="cos_sb", tag="cos_sb")
        sin_sb = keep.tile([P, M_TILES, PAIRS], BF16, name="sin_sb", tag="sin_sb")
        t_even = keep.tile([P, M_TILES, PAIRS, 2], BF16, name="t_even", tag="t_even")
        t_odd = keep.tile([P, M_TILES, PAIRS, 2], BF16, name="t_odd", tag="t_odd")

        def zero_planes(plane, g0, g1):
            nc.vector.memset(plane[:, g0:g1, :].bitcast(I32), 0)

        def load_x_codes(g0, g1, b0=0, b1=2 * TOKENS):
            nc.sync.dma_start(
                out=xc[:, g0:g1, b0:b1].bitcast(I32),
                in_=x_words[g0:g1, :, b0:b1].rearrange("g p b -> p g b").bitcast(I32),
            )

        def load_w_codes(n, g0, g1):
            words, c0 = blocks[n][0], blocks[n][2]
            nc.sync.dma_start(
                out=wc[n][:, g0:g1, :].bitcast(I32),
                in_=words[g0:g1, :, 2 * c0 : 2 * (c0 + N_BLOCK)].rearrange("g p b -> p g b").bitcast(I32),
            )

        def load_scale_quadrant(plane, scales, c0, width, g0, g1, q):
            nc.sync.dma_start(
                out=plane[32 * q : 32 * q + 4, g0:g1, :].bitcast(I32),
                in_=scales[g0:g1, 4 * q : 4 * q + 4, c0 : c0 + width].rearrange("g r n -> r g n").bitcast(I32),
            )

        def load_x_scales(g0, g1):
            for q in (0, 1, 2, 3):
                load_scale_quadrant(xs, x_scales, 0, TOKENS, g0, g1, q)

        def load_w_scales(n, g0, g1):
            for q in (0, 1, 2, 3):
                load_scale_quadrant(ws[n], blocks[n][1], blocks[n][2], N_BLOCK, g0, g1, q)

        nc.gpsimd.memset(xs[:, 0:2, :].bitcast(F32), 0.0)

        zero_planes(ws[0], 0, 2)
        for g0 in range(2, PASSES, 2):
            zero_planes(xs, g0, g0 + 2)
            zero_planes(ws[0], g0, g0 + 2)
        for n in range(1, N_BLOCKS):
            for g0, g1 in W_RUNS:
                zero_planes(ws[n], g0, g1)

        load_x_codes(0, 1)
        load_w_codes(0, 0, 1)
        load_x_scales(0, 2)
        load_w_scales(0, 0, 2)
        load_w_codes(0, 1, 4)
        load_x_codes(1, 2)
        load_x_codes(2, 3)
        load_x_scales(2, 4)
        load_w_scales(0, 2, 4)
        load_x_codes(3, 4)
        for g0 in range(4, PASSES, 2):
            load_x_scales(g0, g0 + 2)
            load_w_scales(0, g0, g0 + 2)
            load_x_codes(g0, g0 + 1)
            load_w_codes(0, g0, g0 + 2)
            load_x_codes(g0 + 1, g0 + 2)
        nc.sync.dma_start(out=cos_sb[:], in_=cos.rearrange("(m p) i -> p m i", p=P))
        nc.sync.dma_start(out=sin_sb[:], in_=sin.rearrange("(m p) i -> p m i", p=P))

        def load_block(n):
            for g0, g1 in W_RUNS:
                load_w_scales(n, g0, g1)
                for g in range(g0, g1, 4):
                    load_w_codes(n, g, g + 4)

        load_block(1)

        nc.vector.tensor_copy(out=t_even[:, :, :, 0], in_=cos_sb[:])
        nc.vector.tensor_copy(out=t_even[:, :, :, 1], in_=sin_sb[:])
        nc.vector.tensor_scalar_mul(out=t_odd[:, :, :, 0], in0=sin_sb[:], scalar1=-1.0)
        nc.vector.tensor_copy(out=t_odd[:, :, :, 1], in_=cos_sb[:])

        order = []
        for g in range(STAGGER_FROM):
            for m in range(M_TILES):
                order.append((m, 0, g))
        for half in (0, 4):
            for g in range(STAGGER_FROM, PASSES):
                for m in range(half, half + 4):
                    order.append((m, 0, g))
        for n in range(1, N_BLOCKS - 1):
            for half in (0, 4):
                for g in range(PASSES):
                    for m in range(half, half + 4):
                        order.append((m, n, g))
        for m in range(M_TILES - 1):
            for g in range(PASSES):
                order.append((m, N_BLOCKS - 1, g))

        full = [P, HEADS_PER_BLOCK, PAIRS, 2]
        acc = {}
        finished = {}
        for m, n, g in order:
            if g == 0:
                acc_mn = psum.tile([P, N_BLOCK], F32, name="acc%d" % m, tag="acc%d" % m)
                acc[m] = acc_mn
            nc.tensor.matmul_mx(
                out=acc[m][:],
                lhsT=xc[:, g, 2 * P * m : 2 * P * (m + 1)].bitcast(FP4X4),
                lhsT_scale=xs[:, g, P * m : P * (m + 1)],
                rhs=wc[n][:, g, :].bitcast(FP4X4),
                rhs_scale=ws[n][:, g, :],
                start=(g == 0),
                stop=(g == PASSES - 1),
            )
            if g < PASSES - 1:
                continue
            dst, h0, rotated = blocks[n][3], blocks[n][4], blocks[n][5]
            rows = dst[0, h0 : h0 + HEADS_PER_BLOCK, P * m : P * (m + 1), :].rearrange("h p l -> p h l")
            a = work.tile(full, F32, name="a", tag="a", bufs=4)
            nc.scalar.copy(out=a[:].rearrange("p h i j -> p (h i j)"), in_=acc[m][:])
            if rotated:
                u = work.tile(full, F32, name="u", tag="u", bufs=4)
                w = work.tile(full, F32, name="w", tag="w", bufs=2)
                nc.vector.tensor_tensor(
                    out=u[:], in0=a[:, :, :, 0:1].to_broadcast(full),
                    in1=t_even[:, m : m + 1, :, :].to_broadcast(full), op=MULT,
                )
                nc.vector.tensor_tensor(
                    out=w[:], in0=a[:, :, :, 1:2].to_broadcast(full),
                    in1=t_odd[:, m : m + 1, :, :].to_broadcast(full), op=MULT,
                )
                nc.vector.tensor_tensor(out=u[:], in0=u[:], in1=w[:], op=ADD)
                nc.sync.dma_start(out=rows, in_=u[:].rearrange("p h i j -> p h (i j)"))
                finished[n] = finished.get(n, 0) + 1
                if finished[n] == M_TILES and n + 2 < N_BLOCKS:
                    load_block(n + 2)
            else:
                nc.sync.dma_start(out=rows, in_=a[:].rearrange("p h i j -> p h (i j)"))

        m = M_TILES - 1
        n = N_BLOCKS - 1
        c0 = 0
        for part, width in enumerate(LAST_WIDTHS):
            bank = (m + part) % M_TILES
            heads = width // P
            acc_h = psum.tile([P, N_BLOCK], F32, name="acc%d" % bank, tag="acc%d" % bank)
            for g in range(PASSES):
                nc.tensor.matmul_mx(
                    out=acc_h[:, 0:width],
                    lhsT=xc[:, g, 2 * P * m : 2 * P * (m + 1)].bitcast(FP4X4),
                    lhsT_scale=xs[:, g, P * m : P * (m + 1)],
                    rhs=wc[n][:, g, 2 * c0 : 2 * (c0 + width)].bitcast(FP4X4),
                    rhs_scale=ws[n][:, g, c0 : c0 + width],
                    start=(g == 0),
                    stop=(g == PASSES - 1),
                )
            a = work.tile(full, F32, name="a", tag="a", bufs=4)
            nc.scalar.copy(out=a[:, 0:heads, :, :].rearrange("p h i j -> p (h i j)"), in_=acc_h[:, 0:width])
            h0 = c0 // P
            nc.sync.dma_start(
                out=out_2[0, h0 : h0 + heads, P * m : P * (m + 1), :].rearrange("h p l -> p h l"),
                in_=a[:, 0:heads, :, :].rearrange("p h i j -> p h (i j)"),
            )
            c0 += width
